import numpy as np
import ml_dtypes

BF16 = ml_dtypes.bfloat16


def bf(x):
    return np.asarray(x, np.float32).astype(BF16)


def f32(x):
    return np.asarray(x, np.float32)


def f64(x):
    return np.asarray(x).astype(np.float64)


def striped(idx):
    return np.tile(idx.reshape(-1, 16).T, (8, 1))


C, S, B, T, N, M, MS = 128, 4096, 4, 512, 2048, 384, 256
SCALE = 100.0 ** 0.25


def pos_term():
    p = np.arange(B, dtype=np.float64)[:, None]
    div = np.exp(np.arange(0, C, 2, dtype=np.float64) * (-np.log(10000.0) / C))
    pe = np.zeros((B, C))
    pe[:, 0::2] = np.sin(p * div)
    pe[:, 1::2] = np.cos(p * div)
    return np.repeat(pe.T, T, axis=1)


def setup_inputs():
    return {"emb": f32(np.random.standard_normal((C, S))), "pos": f32(pos_term()), "w": bf(np.random.standard_normal((C, M)) / np.sqrt(C)), "offs": striped(np.random.permutation(np.tile(np.arange(S), 2))[:N])}


def reference(emb, pos, w, offs):
    idx = offs[:16].T.reshape(-1)
    h = f64(emb)[:, idx] + f64(pos)
    p = f64(w).T @ h
    p[:MS] = p[:MS] / SCALE
    return np.concatenate([h, p], axis=0)

@@ -1,0 +1,62 @@
+import concourse.mybir as mybir
+
+F32, BF16, U16 = mybir.dt.float32, mybir.dt.bfloat16, mybir.dt.uint16
+ADD = mybir.AluOpType.add
+COPY = mybir.ActivationFunctionType.Copy
+
+C = 128
+S = 4096
+N = 2048
+M = 384
+PIECE = 512
+N_PIECES = N // PIECE
+QK_SCALE = 100.0 ** -0.25
+
+FLOPS = 2 * C * M * N
+
+
+def tile_focus_kernel(tc, emb, pos, w, offs, out):
+    nc = tc.nc
+    with (
+        tc.tile_pool(name="held", bufs=1) as held,
+        tc.tile_pool(name="steps", bufs=N_PIECES) as steps,
+        tc.psum_pool(name="banks", bufs=6) as banks,
+    ):
+        offsets = held.tile([C, N // 16], U16, name="offsets")
+        nc.sync.dma_start(offsets[:], offs)
+        pos_tiles = [steps.tile([C, PIECE], F32, name="pos_piece") for _ in range(N_PIECES)]
+        nc.sync.dma_start(pos_tiles[0][:], pos[:, 0:PIECE])
+        table = held.tile([C, S], F32, name="table")
+        nc.sync.dma_start(table[:], emb)
+        weights = held.tile([C, M], BF16, name="weights")
+        nc.sync.dma_start(weights[:], w)
+        for i in range(1, N_PIECES):
+            nc.sync.dma_start(pos_tiles[i][:], pos[:, i * PIECE : (i + 1) * PIECE])
+
+        def embed(i):
+            cols = slice(i * PIECE, (i + 1) * PIECE)
+            h = steps.tile([C, PIECE], F32, name="h")
+            picked = table[:].indirect(offsets[:, i * (PIECE // 16) : (i + 1) * (PIECE // 16)])
+            nc.vector.tensor_tensor(h[:], picked, pos_tiles[i][:], ADD)
+            nc.sync.dma_start(out[0:C, cols], h[:])
+            h_bf = steps.tile([C, PIECE], BF16, name="h_bf")
+            nc.scalar.activation(h_bf[:], h[:], COPY)
+            return h_bf
+
+        def project(i, h_bf):
+            cols = slice(i * PIECE, (i + 1) * PIECE)
+            for block in range(M // C):
+                bank = banks.tile([C, PIECE], F32, name="bank")
+                nc.tensor.matmul(bank[:], weights[:, block * C : (block + 1) * C], h_bf[:])
+                p = steps.tile([C, PIECE], F32, name=f"p{block}")
+                if block < 2:
+                    nc.scalar.activation(p[:], bank[:], COPY, scale=QK_SCALE)
+                else:
+                    nc.vector.tensor_copy(p[:], bank[:])
+                nc.sync.dma_start(out[(block + 1) * C : (block + 2) * C, cols], p[:])
+
+        rounded = [embed(0)]
+        for i in range(N_PIECES):
+            if i + 1 < N_PIECES:
+                rounded.append(embed(i + 1))
+            project(i, rounded[i])

@@ -20,11 +20,11 @@ def tile_focus_kernel(tc, emb, pos, w, offs, out):
     with (
         tc.tile_pool(name="held", bufs=1) as held,
         tc.tile_pool(name="steps", bufs=N_PIECES) as steps,
-        tc.psum_pool(name="banks", bufs=6) as banks,
+        tc.psum_pool(name="banks", bufs=8) as banks,
     ):
         offsets = held.tile([C, N // 16], U16, name="offsets")
         nc.sync.dma_start(offsets[:], offs)
-        pos_tiles = [steps.tile([C, PIECE], F32, name="pos_piece") for _ in range(N_PIECES)]
+        pos_tiles = [steps.tile([C, PIECE], F32, name="pos_piece") for i in range(N_PIECES)]
         nc.sync.dma_start(pos_tiles[0][:], pos[:, 0:PIECE])
         table = held.tile([C, S], F32, name="table")
         nc.sync.dma_start(table[:], emb)
@@ -40,7 +40,7 @@ def tile_focus_kernel(tc, emb, pos, w, offs, out):
             nc.vector.tensor_tensor(h[:], picked, pos_tiles[i][:], ADD)
             nc.sync.dma_start(out[0:C, cols], h[:])
             h_bf = steps.tile([C, PIECE], BF16, name="h_bf")
-            nc.scalar.activation(h_bf[:], h[:], COPY)
+            nc.vector.tensor_copy(h_bf[:], h[:])
             return h_bf
 
         def project(i, h_bf):
@@ -49,10 +49,10 @@ def tile_focus_kernel(tc, emb, pos, w, offs, out):
                 bank = banks.tile([C, PIECE], F32, name="bank")
                 nc.tensor.matmul(bank[:], weights[:, block * C : (block + 1) * C], h_bf[:])
                 p = steps.tile([C, PIECE], F32, name=f"p{block}")
-                if block < 2:
-                    nc.scalar.activation(p[:], bank[:], COPY, scale=QK_SCALE)
-                else:
+                if block == 2 and i >= N_PIECES // 2:
                     nc.vector.tensor_copy(p[:], bank[:])
+                else:
+                    nc.scalar.activation(p[:], bank[:], COPY, scale=QK_SCALE if block < 2 else 1.0)
                 nc.sync.dma_start(out[(block + 1) * C : (block + 2) * C, cols], p[:])
 
         rounded = [embed(0)]

@@ -8,9 +8,12 @@ C = 128
 S = 4096
 N = 2048
 M = 384
-PIECE = 512
-N_PIECES = N // PIECE
+BANK = 512
 QK_SCALE = 100.0 ** -0.25
+STARTS = [0,128,256,512,1024,1536]
+ENDS = STARTS[1:] + [N]
+N_PIECES = len(STARTS)
+AHEAD = 1
 
 FLOPS = 2 * C * M * N
 
@@ -19,44 +22,45 @@ def tile_focus_kernel(tc, emb, pos, w, offs, out):
     nc = tc.nc
     with (
         tc.tile_pool(name="held", bufs=1) as held,
-        tc.tile_pool(name="steps", bufs=N_PIECES) as steps,
         tc.psum_pool(name="banks", bufs=8) as banks,
     ):
         offsets = held.tile([C, N // 16], U16, name="offsets")
         nc.sync.dma_start(offsets[:], offs)
-        pos_tiles = [steps.tile([C, PIECE], F32, name="pos_piece") for i in range(N_PIECES)]
-        nc.sync.dma_start(pos_tiles[0][:], pos[:, 0:PIECE])
+        pos_sb = held.tile([C, N], F32, name="pos_sb")
+        nc.sync.dma_start(pos_sb[:, 0 : ENDS[0]], pos[:, 0 : ENDS[0]])
         table = held.tile([C, S], F32, name="table")
         nc.sync.dma_start(table[:], emb)
         weights = held.tile([C, M], BF16, name="weights")
         nc.sync.dma_start(weights[:], w)
         for i in range(1, N_PIECES):
-            nc.sync.dma_start(pos_tiles[i][:], pos[:, i * PIECE : (i + 1) * PIECE])
+            nc.sync.dma_start(pos_sb[:, STARTS[i] : ENDS[i]], pos[:, STARTS[i] : ENDS[i]])
+
+        h = held.tile([C, N], F32, name="h")
+        h_bf = held.tile([C, N], BF16, name="h_bf")
+        p = held.tile([C, M // C, N], F32, name="p")
 
         def embed(i):
-            cols = slice(i * PIECE, (i + 1) * PIECE)
-            h = steps.tile([C, PIECE], F32, name="h")
-            picked = table[:].indirect(offsets[:, i * (PIECE // 16) : (i + 1) * (PIECE // 16)])
-            nc.vector.tensor_tensor(h[:], picked, pos_tiles[i][:], ADD)
-            nc.sync.dma_start(out[0:C, cols], h[:])
-            h_bf = steps.tile([C, PIECE], BF16, name="h_bf")
-            nc.vector.tensor_copy(h_bf[:], h[:])
-            return h_bf
+            cols = slice(STARTS[i], ENDS[i])
+            picked = table[:].indirect(offsets[:, STARTS[i] // 16 : ENDS[i] // 16])
+            nc.vector.tensor_tensor(h[:, cols], picked, pos_sb[:, cols], ADD)
+            nc.sync.dma_start(out[0:C, cols], h[:, cols])
+            nc.scalar.activation(h_bf[:, cols], h[:, cols], COPY)
 
-        def project(i, h_bf):
-            cols = slice(i * PIECE, (i + 1) * PIECE)
+        def project(i):
+            cols = slice(STARTS[i], ENDS[i])
+            width = ENDS[i] - STARTS[i]
             for block in range(M // C):
-                bank = banks.tile([C, PIECE], F32, name="bank")
-                nc.tensor.matmul(bank[:], weights[:, block * C : (block + 1) * C], h_bf[:])
-                p = steps.tile([C, PIECE], F32, name=f"p{block}")
-                if block == 2 and i >= N_PIECES // 2:
-                    nc.vector.tensor_copy(p[:], bank[:])
+                bank = banks.tile([C, BANK], F32, name="bank")
+                nc.tensor.matmul(bank[:, 0:width], weights[:, block * C : (block + 1) * C], h_bf[:, cols])
+                if block == 2 and True:
+                    nc.vector.tensor_copy(p[:, block, cols], bank[:, 0:width])
                 else:
-                    nc.scalar.activation(p[:], bank[:], COPY, scale=QK_SCALE if block < 2 else 1.0)
-                nc.sync.dma_start(out[(block + 1) * C : (block + 2) * C, cols], p[:])
+                    nc.scalar.activation(p[:, block, cols], bank[:, 0:width], COPY, scale=QK_SCALE if block < 2 else 1.0)
+                nc.sync.dma_start(out[(block + 1) * C : (block + 2) * C, cols], p[:, block, cols])
 
-        rounded = [embed(0)]
+        for i in range(AHEAD):
+            embed(i)
         for i in range(N_PIECES):
-            if i + 1 < N_PIECES:
-                rounded.append(embed(i + 1))
-            project(i, rounded[i])
+            if i + AHEAD < N_PIECES:
+                embed(i + AHEAD)
+            project(i)

@@ -30,11 +30,12 @@ def tile_focus_kernel(tc, emb, pos, w, offs, out):
         nc.sync.dma_start(pos_sb[:, 0 : ENDS[0]], pos[:, 0 : ENDS[0]])
         table = held.tile([C, S], F32, name="table")
         nc.sync.dma_start(table[:], emb)
+        nc.sync.dma_start(pos_sb[:, ENDS[0] : BANK], pos[:, ENDS[0] : BANK])
         weights = held.tile([C, M], BF16, name="weights")
         nc.sync.dma_start(weights[:], w)
-        for i in range(1, N_PIECES):
-            nc.sync.dma_start(pos_sb[:, STARTS[i] : ENDS[i]], pos[:, STARTS[i] : ENDS[i]])
+        nc.sync.dma_start(pos_sb[:, BANK:N], pos[:, BANK:N])
 
+        out_blocks = out.rearrange("(b c) n -> c b n", c=C)
         h = held.tile([C, N], F32, name="h")
         h_bf = held.tile([C, N], BF16, name="h_bf")
         p = held.tile([C, M // C, N], F32, name="p")
@@ -56,7 +57,10 @@ def tile_focus_kernel(tc, emb, pos, w, offs, out):
                     nc.vector.tensor_copy(p[:, block, cols], bank[:, 0:width])
                 else:
                     nc.scalar.activation(p[:, block, cols], bank[:, 0:width], COPY, scale=QK_SCALE if block < 2 else 1.0)
-                nc.sync.dma_start(out[(block + 1) * C : (block + 2) * C, cols], p[:, block, cols])
+                if i == N_PIECES - 1:
+                    nc.sync.dma_start(out_blocks[:, block + 1, cols], p[:, block, cols])
+            if i < N_PIECES - 1:
+                nc.sync.dma_start(out_blocks[:, 1:, cols], p[:, :, cols])
 
         for i in range(AHEAD):
             embed(i)

@@ -13,6 +13,7 @@ QK_SCALE = 100.0 ** -0.25
 STARTS = [0,128,256,512,1024,1536]
 ENDS = STARTS[1:] + [N]
 N_PIECES = len(STARTS)
+POS_CUTS = [128,512,1024]
 AHEAD = 1
 
 FLOPS = 2 * C * M * N
@@ -27,13 +28,13 @@ def tile_focus_kernel(tc, emb, pos, w, offs, out):
         offsets = held.tile([C, N // 16], U16, name="offsets")
         nc.sync.dma_start(offsets[:], offs)
         pos_sb = held.tile([C, N], F32, name="pos_sb")
-        nc.sync.dma_start(pos_sb[:, 0 : ENDS[0]], pos[:, 0 : ENDS[0]])
+        nc.sync.dma_start(pos_sb[:, 0 : POS_CUTS[0]], pos[:, 0 : POS_CUTS[0]])
         table = held.tile([C, S], F32, name="table")
         nc.sync.dma_start(table[:], emb)
-        nc.sync.dma_start(pos_sb[:, ENDS[0] : BANK], pos[:, ENDS[0] : BANK])
         weights = held.tile([C, M], BF16, name="weights")
         nc.sync.dma_start(weights[:], w)
-        nc.sync.dma_start(pos_sb[:, BANK:N], pos[:, BANK:N])
+        for lo, hi in zip(POS_CUTS, POS_CUTS[1:] + [N]):
+            nc.sync.dma_start(pos_sb[:, lo:hi], pos[:, lo:hi])
 
         out_blocks = out.rearrange("(b c) n -> c b n", c=C)
         h = held.tile([C, N], F32, name="h")
@@ -44,8 +45,8 @@ def tile_focus_kernel(tc, emb, pos, w, offs, out):
             cols = slice(STARTS[i], ENDS[i])
             picked = table[:].indirect(offsets[:, STARTS[i] // 16 : ENDS[i] // 16])
             nc.vector.tensor_tensor(h[:, cols], picked, pos_sb[:, cols], ADD)
-            nc.sync.dma_start(out[0:C, cols], h[:, cols])
             nc.scalar.activation(h_bf[:, cols], h[:, cols], COPY)
+            nc.scalar.dma_start(out[0:C, cols], h[:, cols])
 
         def project(i):
             cols = slice(STARTS[i], ENDS[i])
@@ -57,10 +58,7 @@ def tile_focus_kernel(tc, emb, pos, w, offs, out):
                     nc.vector.tensor_copy(p[:, block, cols], bank[:, 0:width])
                 else:
                     nc.scalar.activation(p[:, block, cols], bank[:, 0:width], COPY, scale=QK_SCALE if block < 2 else 1.0)
-                if i == N_PIECES - 1:
-                    nc.sync.dma_start(out_blocks[:, block + 1, cols], p[:, block, cols])
-            if i < N_PIECES - 1:
-                nc.sync.dma_start(out_blocks[:, 1:, cols], p[:, :, cols])
+            nc.sync.dma_start(out_blocks[:, 1:, cols], p[:, :, cols])
 
         for i in range(AHEAD):
             embed(i)

@@ -45,8 +45,8 @@ def tile_focus_kernel(tc, emb, pos, w, offs, out):
             cols = slice(STARTS[i], ENDS[i])
             picked = table[:].indirect(offsets[:, STARTS[i] // 16 : ENDS[i] // 16])
             nc.vector.tensor_tensor(h[:, cols], picked, pos_sb[:, cols], ADD)
+            nc.sync.dma_start(out[0:C, cols], h[:, cols])
             nc.scalar.activation(h_bf[:, cols], h[:, cols], COPY)
-            nc.scalar.dma_start(out[0:C, cols], h[:, cols])
 
         def project(i):
             cols = slice(STARTS[i], ENDS[i])

@@ -13,7 +13,6 @@ QK_SCALE = 100.0 ** -0.25
 STARTS = [0,128,256,512,1024,1536]
 ENDS = STARTS[1:] + [N]
 N_PIECES = len(STARTS)
-POS_CUTS = [128,512,1024]
 AHEAD = 1
 
 FLOPS = 2 * C * M * N
@@ -28,15 +27,14 @@ def tile_focus_kernel(tc, emb, pos, w, offs, out):
         offsets = held.tile([C, N // 16], U16, name="offsets")
         nc.sync.dma_start(offsets[:], offs)
         pos_sb = held.tile([C, N], F32, name="pos_sb")
-        nc.sync.dma_start(pos_sb[:, 0 : POS_CUTS[0]], pos[:, 0 : POS_CUTS[0]])
+        nc.sync.dma_start(pos_sb[:, 0 : ENDS[0]], pos[:, 0 : ENDS[0]])
         table = held.tile([C, S], F32, name="table")
         nc.sync.dma_start(table[:], emb)
+        nc.sync.dma_start(pos_sb[:, ENDS[0] : BANK], pos[:, ENDS[0] : BANK])
         weights = held.tile([C, M], BF16, name="weights")
         nc.sync.dma_start(weights[:], w)
-        for lo, hi in zip(POS_CUTS, POS_CUTS[1:] + [N]):
-            nc.sync.dma_start(pos_sb[:, lo:hi], pos[:, lo:hi])
+        nc.sync.dma_start(pos_sb[:, BANK:N], pos[:, BANK:N])
 
-        out_blocks = out.rearrange("(b c) n -> c b n", c=C)
         h = held.tile([C, N], F32, name="h")
         h_bf = held.tile([C, N], BF16, name="h_bf")
         p = held.tile([C, M // C, N], F32, name="p")
@@ -58,7 +56,7 @@ def tile_focus_kernel(tc, emb, pos, w, offs, out):
                     nc.vector.tensor_copy(p[:, block, cols], bank[:, 0:width])
                 else:
                     nc.scalar.activation(p[:, block, cols], bank[:, 0:width], COPY, scale=QK_SCALE if block < 2 else 1.0)
-            nc.sync.dma_start(out_blocks[:, 1:, cols], p[:, :, cols])
+                nc.sync.dma_start(out[(block + 1) * C : (block + 2) * C, cols], p[:, block, cols])
 
         for i in range(AHEAD):
             embed(i)

@@ -7,6 +7,9 @@ COPY = mybir.ActivationFunctionType.Copy
 C = 128
 S = 4096
 N = 2048
+B = 4
+T = 512
+HEAD = 8
 M = 384
 BANK = 512
 QK_SCALE = 100.0 ** -0.25
@@ -26,14 +29,18 @@ def tile_focus_kernel(tc, emb, pos, w, offs, out):
     ):
         offsets = held.tile([C, N // 16], U16, name="offsets")
         nc.sync.dma_start(offsets[:], offs)
-        pos_sb = held.tile([C, N], F32, name="pos_sb")
-        nc.sync.dma_start(pos_sb[:, 0 : ENDS[0]], pos[:, 0 : ENDS[0]])
+        pos_head = held.tile([C, B, HEAD], F32, name="pos_head")
+        nc.sync.dma_start(pos_head[:], pos.rearrange("c (b t) -> c b t", b=B)[:, :, 0:HEAD])
         table = held.tile([C, S], F32, name="table")
         nc.sync.dma_start(table[:], emb)
-        nc.sync.dma_start(pos_sb[:, ENDS[0] : BANK], pos[:, ENDS[0] : BANK])
         weights = held.tile([C, M], BF16, name="weights")
         nc.sync.dma_start(weights[:], w)
-        nc.sync.dma_start(pos_sb[:, BANK:N], pos[:, BANK:N])
+
+        pos_sb = held.tile([C, N], F32, name="pos_sb")
+        nc.vector.tensor_copy(
+            pos_sb[:].rearrange("c (b t) -> c b t", b=B),
+            pos_head[:, :, 0:1].to_broadcast([C, B, T]),
+        )
 
         h = held.tile([C, N], F32, name="h")
         h_bf = held.tile([C, N], BF16, name="h_bf")

@@ -10,22 +10,19 @@ N = 2048
 B = 4
 T = 512
 HEAD = 8
-M = 384
-BANK = 512
 QK_SCALE = 100.0 ** -0.25
-STARTS = [0,128,256,512,1024,1536]
-ENDS = STARTS[1:] + [N]
-N_PIECES = len(STARTS)
-AHEAD = 1
+PIECE = 256
+N_PIECES = N // PIECE
+VECTOR_EMPTIES_FROM = N_PIECES // 2
 
-FLOPS = 2 * C * M * N
+FLOPS = 2 * C * 3 * C * N
 
 
 def tile_focus_kernel(tc, emb, pos, w, offs, out):
     nc = tc.nc
     with (
         tc.tile_pool(name="held", bufs=1) as held,
-        tc.psum_pool(name="banks", bufs=8) as banks,
+        tc.psum_pool(name="banks", bufs=4) as banks,
     ):
         offsets = held.tile([C, N // 16], U16, name="offsets")
         nc.sync.dma_start(offsets[:], offs)
@@ -33,8 +30,8 @@ def tile_focus_kernel(tc, emb, pos, w, offs, out):
         nc.sync.dma_start(pos_head[:], pos.rearrange("c (b t) -> c b t", b=B)[:, :, 0:HEAD])
         table = held.tile([C, S], F32, name="table")
         nc.sync.dma_start(table[:], emb)
-        weights = held.tile([C, M], BF16, name="weights")
-        nc.sync.dma_start(weights[:], w)
+        weights = held.tile([C, 3, C], BF16, name="weights")
+        nc.sync.dma_start(weights[:], w.rearrange("c (m d) -> c m d", m=3))
 
         pos_sb = held.tile([C, N], F32, name="pos_sb")
         nc.vector.tensor_copy(
@@ -44,30 +41,24 @@ def tile_focus_kernel(tc, emb, pos, w, offs, out):
 
         h = held.tile([C, N], F32, name="h")
         h_bf = held.tile([C, N], BF16, name="h_bf")
-        p = held.tile([C, M // C, N], F32, name="p")
+        p = held.tile([C, 3, N], F32, name="p")
+        out_p = out[C : 4 * C, :].rearrange("(m c) j -> c m j", m=3)
 
-        def embed(i):
-            cols = slice(STARTS[i], ENDS[i])
-            picked = table[:].indirect(offsets[:, STARTS[i] // 16 : ENDS[i] // 16])
+        for i in range(N_PIECES):
+            cols = slice(i * PIECE, (i + 1) * PIECE)
+            picked = table[:].indirect(offsets[:, i * PIECE // 16 : (i + 1) * PIECE // 16])
             nc.vector.tensor_tensor(h[:, cols], picked, pos_sb[:, cols], ADD)
             nc.sync.dma_start(out[0:C, cols], h[:, cols])
-            nc.scalar.activation(h_bf[:, cols], h[:, cols], COPY)
-
-        def project(i):
-            cols = slice(STARTS[i], ENDS[i])
-            width = ENDS[i] - STARTS[i]
-            for block in range(M // C):
-                bank = banks.tile([C, BANK], F32, name="bank")
-                nc.tensor.matmul(bank[:, 0:width], weights[:, block * C : (block + 1) * C], h_bf[:, cols])
-                if block == 2 and True:
-                    nc.vector.tensor_copy(p[:, block, cols], bank[:, 0:width])
-                else:
-                    nc.scalar.activation(p[:, block, cols], bank[:, 0:width], COPY, scale=QK_SCALE if block < 2 else 1.0)
-                nc.sync.dma_start(out[(block + 1) * C : (block + 2) * C, cols], p[:, block, cols])
-
-        for i in range(AHEAD):
-            embed(i)
-        for i in range(N_PIECES):
-            if i + AHEAD < N_PIECES:
-                embed(i + AHEAD)
-            project(i)
+            nc.vector.tensor_copy(h_bf[:, cols], h[:, cols])
+            qk_bank = banks.tile([C, 2, PIECE], F32, name="qk_bank")
+            v_bank = banks.tile([C, PIECE], F32, name="v_bank")
+            nc.tensor.matmul(qk_bank[:, 0, :], weights[:, 0, :], h_bf[:, cols])
+            nc.tensor.matmul(qk_bank[:, 1, :], weights[:, 1, :], h_bf[:, cols])
+            nc.tensor.matmul(v_bank[:], weights[:, 2, :], h_bf[:, cols])
+            nc.scalar.activation(p[:, 0:2, cols], qk_bank[:], COPY, scale=QK_SCALE)
+            nc.sync.dma_start(out_p[:, 0:2, cols], p[:, 0:2, cols])
+            if i < VECTOR_EMPTIES_FROM:
+                nc.scalar.activation(p[:, 2, cols], v_bank[:], COPY)
+            else:
+                nc.vector.tensor_copy(p[:, 2, cols], v_bank[:])
+            nc.sync.dma_start(out_p[:, 2, cols], p[:, 2, cols])

@@ -12,8 +12,11 @@ T = 512
 HEAD = 8
 QK_SCALE = 100.0 ** -0.25
 PIECE = 256
-N_PIECES = N // PIECE
-VECTOR_EMPTIES_FROM = N_PIECES // 2
+WIDTHS = [PIECE // 2, PIECE // 2] + [PIECE] * (N // PIECE - 1)
+STARTS = [sum(WIDTHS[:i]) for i in range(len(WIDTHS))]
+N_PIECES = len(WIDTHS)
+SCALAR_ROUNDS = 3
+VECTOR_EMPTIES_FROM = N_PIECES - 3
 
 FLOPS = 2 * C * 3 * C * N
 
@@ -45,20 +48,24 @@ def tile_focus_kernel(tc, emb, pos, w, offs, out):
         out_p = out[C : 4 * C, :].rearrange("(m c) j -> c m j", m=3)
 
         for i in range(N_PIECES):
-            cols = slice(i * PIECE, (i + 1) * PIECE)
-            picked = table[:].indirect(offsets[:, i * PIECE // 16 : (i + 1) * PIECE // 16])
+            width = WIDTHS[i]
+            cols = slice(STARTS[i], STARTS[i] + width)
+            picked = table[:].indirect(offsets[:, cols.start // 16 : cols.stop // 16])
             nc.vector.tensor_tensor(h[:, cols], picked, pos_sb[:, cols], ADD)
             nc.sync.dma_start(out[0:C, cols], h[:, cols])
-            nc.vector.tensor_copy(h_bf[:, cols], h[:, cols])
+            if i < SCALAR_ROUNDS:
+                nc.scalar.activation(h_bf[:, cols], h[:, cols], COPY)
+            else:
+                nc.vector.tensor_copy(h_bf[:, cols], h[:, cols])
             qk_bank = banks.tile([C, 2, PIECE], F32, name="qk_bank")
             v_bank = banks.tile([C, PIECE], F32, name="v_bank")
-            nc.tensor.matmul(qk_bank[:, 0, :], weights[:, 0, :], h_bf[:, cols])
-            nc.tensor.matmul(qk_bank[:, 1, :], weights[:, 1, :], h_bf[:, cols])
-            nc.tensor.matmul(v_bank[:], weights[:, 2, :], h_bf[:, cols])
-            nc.scalar.activation(p[:, 0:2, cols], qk_bank[:], COPY, scale=QK_SCALE)
+            nc.tensor.matmul(qk_bank[:, 0, 0:width], weights[:, 0, :], h_bf[:, cols])
+            nc.tensor.matmul(qk_bank[:, 1, 0:width], weights[:, 1, :], h_bf[:, cols])
+            nc.tensor.matmul(v_bank[:, 0:width], weights[:, 2, :], h_bf[:, cols])
+            nc.scalar.activation(p[:, 0:2, cols], qk_bank[:, :, 0:width], COPY, scale=QK_SCALE)
             nc.sync.dma_start(out_p[:, 0:2, cols], p[:, 0:2, cols])
             if i < VECTOR_EMPTIES_FROM:
-                nc.scalar.activation(p[:, 2, cols], v_bank[:], COPY)
+                nc.scalar.activation(p[:, 2, cols], v_bank[:, 0:width], COPY)
             else:
-                nc.vector.tensor_copy(p[:, 2, cols], v_bank[:])
+                nc.vector.tensor_copy(p[:, 2, cols], v_bank[:, 0:width])
             nc.sync.dma_start(out_p[:, 2, cols], p[:, 2, cols])

@@ -16,7 +16,7 @@ WIDTHS = [PIECE // 2, PIECE // 2] + [PIECE] * (N // PIECE - 1)
 STARTS = [sum(WIDTHS[:i]) for i in range(len(WIDTHS))]
 N_PIECES = len(WIDTHS)
 SCALAR_ROUNDS = 3
-VECTOR_EMPTIES_FROM = N_PIECES - 3
+VECTOR_EMPTIES_FROM = N_PIECES - 0
 
 FLOPS = 2 * C * 3 * C * N
 

import concourse.mybir as mybir

F32, BF16, U16 = mybir.dt.float32, mybir.dt.bfloat16, mybir.dt.uint16
ADD = mybir.AluOpType.add
COPY = mybir.ActivationFunctionType.Copy

C = 128
S = 4096
N = 2048
B = 4
T = 512
HEAD = 8
QK_SCALE = 100.0 ** -0.25
PIECE = 256
WIDTHS = [PIECE // 2, PIECE // 2] + [PIECE] * (N // PIECE - 1)
STARTS = [sum(WIDTHS[:i]) for i in range(len(WIDTHS))]
N_PIECES = len(WIDTHS)
SCALAR_ROUNDS = 3
VECTOR_EMPTIES_FROM = N_PIECES - 0

FLOPS = 2 * C * 3 * C * N


def tile_focus_kernel(tc, emb, pos, w, offs, out):
    nc = tc.nc
    with (
        tc.tile_pool(name="held", bufs=1) as held,
        tc.psum_pool(name="banks", bufs=4) as banks,
    ):
        offsets = held.tile([C, N // 16], U16, name="offsets")
        nc.sync.dma_start(offsets[:], offs)
        pos_head = held.tile([C, B, HEAD], F32, name="pos_head")
        nc.sync.dma_start(pos_head[:], pos.rearrange("c (b t) -> c b t", b=B)[:, :, 0:HEAD])
        table = held.tile([C, S], F32, name="table")
        nc.sync.dma_start(table[:], emb)
        weights = held.tile([C, 3, C], BF16, name="weights")
        nc.sync.dma_start(weights[:], w.rearrange("c (m d) -> c m d", m=3))

        pos_sb = held.tile([C, N], F32, name="pos_sb")
        nc.vector.tensor_copy(
            pos_sb[:].rearrange("c (b t) -> c b t", b=B),
            pos_head[:, :, 0:1].to_broadcast([C, B, T]),
        )

        h = held.tile([C, N], F32, name="h")
        h_bf = held.tile([C, N], BF16, name="h_bf")
        p = held.tile([C, 3, N], F32, name="p")
        out_p = out[C : 4 * C, :].rearrange("(m c) j -> c m j", m=3)

        for i in range(N_PIECES):
            width = WIDTHS[i]
            cols = slice(STARTS[i], STARTS[i] + width)
            picked = table[:].indirect(offsets[:, cols.start // 16 : cols.stop // 16])
            nc.vector.tensor_tensor(h[:, cols], picked, pos_sb[:, cols], ADD)
            nc.sync.dma_start(out[0:C, cols], h[:, cols])
            if i < SCALAR_ROUNDS:
                nc.scalar.activation(h_bf[:, cols], h[:, cols], COPY)
            else:
                nc.vector.tensor_copy(h_bf[:, cols], h[:, cols])
            qk_bank = banks.tile([C, 2, PIECE], F32, name="qk_bank")
            v_bank = banks.tile([C, PIECE], F32, name="v_bank")
            nc.tensor.matmul(qk_bank[:, 0, 0:width], weights[:, 0, :], h_bf[:, cols])
            nc.tensor.matmul(qk_bank[:, 1, 0:width], weights[:, 1, :], h_bf[:, cols])
            nc.tensor.matmul(v_bank[:, 0:width], weights[:, 2, :], h_bf[:, cols])
            nc.scalar.activation(p[:, 0:2, cols], qk_bank[:, :, 0:width], COPY, scale=QK_SCALE)
            nc.sync.dma_start(out_p[:, 0:2, cols], p[:, 0:2, cols])
            if i < VECTOR_EMPTIES_FROM:
                nc.scalar.activation(p[:, 2, cols], v_bank[:, 0:width], COPY)
            else:
                nc.vector.tensor_copy(p[:, 2, cols], v_bank[:, 0:width])
            nc.sync.dma_start(out_p[:, 2, cols], p[:, 2, cols])
